import numpy as np
import ml_dtypes

BF16 = ml_dtypes.bfloat16


def bf(x):
    return np.asarray(x, np.float32).astype(BF16)


def f32(x):
    return np.asarray(x, np.float32)


def f64(x):
    return np.asarray(x).astype(np.float64)


def striped(idx):
    return np.tile(idx.reshape(-1, 16).T, (8, 1))


C, S, Q, K, N, H = 512, 1024, 2, 2, 4096, 512


def setup_inputs():
    hg = f32(np.random.uniform(0.0, 1.0, (C, S)))
    member = f32(0.5 + np.random.uniform(0.0, 1.0, (1, N)))
    idx = np.concatenate([np.random.permutation(S)[:H] for _ in range(N // H)])
    return {"hg": hg, "member": member, "offs": striped(idx)}


def reference(hg, member, offs):
    idx = offs[:16].T.reshape(-1)
    t = f64(hg)[:, idx] * f64(member)
    return t.reshape(C, Q, K, S).max(axis=2).reshape(C, Q * S)

@@ -1,0 +1,56 @@
+import concourse.mybir as mybir
+
+F32 = mybir.dt.float32
+U16 = mybir.dt.uint16
+MULT = mybir.AluOpType.mult
+MAX = mybir.AluOpType.max
+
+P = 128
+NODES = 512
+EDGES = 1024
+COALITIONS = 2
+MEMBERS = 2
+LIST = COALITIONS * MEMBERS * EDGES
+PER_COLUMN = 16
+
+
+def tile_position_game_kernel(tc, hg, member, offs, out):
+    nc = tc.nc
+    blocks = NODES // P
+    pieces = COALITIONS * MEMBERS
+    with (
+        tc.tile_pool(name="held", bufs=1) as held,
+        tc.tile_pool(name="work", bufs=3) as work,
+    ):
+        offsets = held.tile([P, LIST // PER_COLUMN], U16, name="offsets")
+        nc.sync.dma_start(offsets[:], offs)
+
+        weights = []
+        for j in range(pieces):
+            weight = held.tile([P, EDGES], F32, name=f"weight{j}")
+            nc.sync.dma_start(weight[:], member[0, j * EDGES : (j + 1) * EDGES].partition_broadcast(P))
+            weights.append(weight)
+
+        windows = []
+        for b in range(blocks):
+            window = held.tile([P, EDGES], F32, name=f"window{b}")
+            nc.scalar.dma_start(window[:], hg[b * P : (b + 1) * P, :])
+            windows.append(window)
+
+        for b in range(blocks):
+            for q in range(COALITIONS):
+                picked = []
+                for k in range(MEMBERS):
+                    j = q * MEMBERS + k
+                    columns = EDGES // PER_COLUMN
+                    product = work.tile([P, EDGES], F32, name=f"product{k}")
+                    nc.vector.tensor_tensor(
+                        product[:],
+                        windows[b][:].indirect(offsets[:, j * columns : (j + 1) * columns]),
+                        weights[j][:],
+                        MULT,
+                    )
+                    picked.append(product)
+                union = work.tile([P, EDGES], F32, name="union")
+                nc.vector.tensor_tensor(union[:], picked[0][:], picked[1][:], MAX)
+                nc.sync.dma_start(out[b * P : (b + 1) * P, q * EDGES : (q + 1) * EDGES], union[:])

@@ -18,6 +18,7 @@ def tile_position_game_kernel(tc, hg, member, offs, out):
     nc = tc.nc
     blocks = NODES // P
     pieces = COALITIONS * MEMBERS
+    columns = EDGES // PER_COLUMN
     with (
         tc.tile_pool(name="held", bufs=1) as held,
         tc.tile_pool(name="work", bufs=3) as work,
@@ -37,20 +38,30 @@ def tile_position_game_kernel(tc, hg, member, offs, out):
             nc.scalar.dma_start(window[:], hg[b * P : (b + 1) * P, :])
             windows.append(window)
 
-        for b in range(blocks):
-            for q in range(COALITIONS):
-                picked = []
-                for k in range(MEMBERS):
-                    j = q * MEMBERS + k
-                    columns = EDGES // PER_COLUMN
-                    product = work.tile([P, EDGES], F32, name=f"product{k}")
-                    nc.vector.tensor_tensor(
-                        product[:],
-                        windows[b][:].indirect(offsets[:, j * columns : (j + 1) * columns]),
-                        weights[j][:],
-                        MULT,
-                    )
-                    picked.append(product)
-                union = work.tile([P, EDGES], F32, name="union")
-                nc.vector.tensor_tensor(union[:], picked[0][:], picked[1][:], MAX)
-                nc.sync.dma_start(out[b * P : (b + 1) * P, q * EDGES : (q + 1) * EDGES], union[:])
+        def look_up(b, q):
+            products = []
+            for k in range(MEMBERS):
+                j = q * MEMBERS + k
+                product = work.tile([P, EDGES], F32, name=f"product{k}")
+                nc.vector.tensor_tensor(
+                    product[:],
+                    windows[b][:].indirect(offsets[:, j * columns : (j + 1) * columns]),
+                    weights[j][:],
+                    MULT,
+                )
+                products.append(product)
+            return products
+
+        def unite(b, q, products):
+            union = work.tile([P, EDGES], F32, name="union")
+            nc.vector.tensor_tensor(union[:], products[0][:], products[1][:], MAX)
+            nc.sync.dma_start(out[b * P : (b + 1) * P, q * EDGES : (q + 1) * EDGES], union[:])
+
+        steps = [(b, q) for b in range(blocks) for q in range(COALITIONS)]
+        waiting = None
+        for b, q in steps:
+            products = look_up(b, q)
+            if waiting is not None:
+                unite(*waiting)
+            waiting = (b, q, products)
+        unite(*waiting)

@@ -12,13 +12,13 @@ COALITIONS = 2
 MEMBERS = 2
 LIST = COALITIONS * MEMBERS * EDGES
 PER_COLUMN = 16
+PIECE = 512
+RUNS = EDGES // PIECE
 
 
 def tile_position_game_kernel(tc, hg, member, offs, out):
     nc = tc.nc
     blocks = NODES // P
-    pieces = COALITIONS * MEMBERS
-    columns = EDGES // PER_COLUMN
     with (
         tc.tile_pool(name="held", bufs=1) as held,
         tc.tile_pool(name="work", bufs=3) as work,
@@ -26,11 +26,17 @@ def tile_position_game_kernel(tc, hg, member, offs, out):
         offsets = held.tile([P, LIST // PER_COLUMN], U16, name="offsets")
         nc.sync.dma_start(offsets[:], offs)
 
-        weights = []
-        for j in range(pieces):
-            weight = held.tile([P, EDGES], F32, name=f"weight{j}")
-            nc.sync.dma_start(weight[:], member[0, j * EDGES : (j + 1) * EDGES].partition_broadcast(P))
-            weights.append(weight)
+        def first_entry(q, k, r):
+            return (q * MEMBERS + k) * EDGES + r * PIECE
+
+        weights = {}
+        for q in range(COALITIONS):
+            for r in range(RUNS):
+                for k in range(MEMBERS):
+                    start = first_entry(q, k, r)
+                    weight = held.tile([P, PIECE], F32, name=f"weight{start}")
+                    nc.sync.dma_start(weight[:], member[0, start : start + PIECE].partition_broadcast(P))
+                    weights[start] = weight
 
         windows = []
         for b in range(blocks):
@@ -38,30 +44,31 @@ def tile_position_game_kernel(tc, hg, member, offs, out):
             nc.scalar.dma_start(window[:], hg[b * P : (b + 1) * P, :])
             windows.append(window)
 
-        def look_up(b, q):
+        def look_up(b, q, r):
             products = []
             for k in range(MEMBERS):
-                j = q * MEMBERS + k
-                product = work.tile([P, EDGES], F32, name=f"product{k}")
+                start = first_entry(q, k, r)
+                product = work.tile([P, PIECE], F32, name=f"product{k}")
                 nc.vector.tensor_tensor(
                     product[:],
-                    windows[b][:].indirect(offsets[:, j * columns : (j + 1) * columns]),
-                    weights[j][:],
+                    windows[b][:].indirect(offsets[:, start // PER_COLUMN : (start + PIECE) // PER_COLUMN]),
+                    weights[start][:],
                     MULT,
                 )
                 products.append(product)
             return products
 
-        def unite(b, q, products):
-            union = work.tile([P, EDGES], F32, name="union")
+        def unite(b, q, r, products):
+            union = work.tile([P, PIECE], F32, name="union")
             nc.vector.tensor_tensor(union[:], products[0][:], products[1][:], MAX)
-            nc.sync.dma_start(out[b * P : (b + 1) * P, q * EDGES : (q + 1) * EDGES], union[:])
+            column = q * EDGES + r * PIECE
+            nc.sync.dma_start(out[b * P : (b + 1) * P, column : column + PIECE], union[:])
 
-        steps = [(b, q) for b in range(blocks) for q in range(COALITIONS)]
+        steps = [(b, q, r) for b in range(blocks) for q in range(COALITIONS) for r in range(RUNS)]
         waiting = None
-        for b, q in steps:
-            products = look_up(b, q)
+        for b, q, r in steps:
+            products = look_up(b, q, r)
             if waiting is not None:
                 unite(*waiting)
-            waiting = (b, q, products)
+            waiting = (b, q, r, products)
         unite(*waiting)

@@ -12,13 +12,13 @@ COALITIONS = 2
 MEMBERS = 2
 LIST = COALITIONS * MEMBERS * EDGES
 PER_COLUMN = 16
-PIECE = 512
-RUNS = EDGES // PIECE
 
 
 def tile_position_game_kernel(tc, hg, member, offs, out):
     nc = tc.nc
     blocks = NODES // P
+    pieces = COALITIONS * MEMBERS
+    columns = EDGES // PER_COLUMN
     with (
         tc.tile_pool(name="held", bufs=1) as held,
         tc.tile_pool(name="work", bufs=3) as work,
@@ -26,49 +26,45 @@ def tile_position_game_kernel(tc, hg, member, offs, out):
         offsets = held.tile([P, LIST // PER_COLUMN], U16, name="offsets")
         nc.sync.dma_start(offsets[:], offs)
 
-        def first_entry(q, k, r):
-            return (q * MEMBERS + k) * EDGES + r * PIECE
 
-        weights = {}
-        for q in range(COALITIONS):
-            for r in range(RUNS):
-                for k in range(MEMBERS):
-                    start = first_entry(q, k, r)
-                    weight = held.tile([P, PIECE], F32, name=f"weight{start}")
-                    nc.sync.dma_start(weight[:], member[0, start : start + PIECE].partition_broadcast(P))
-                    weights[start] = weight
+        weights = []
+        for j in range(pieces):
+            weight = held.tile([P, EDGES], F32, name=f"weight{j}")
+            queue = nc.sync if j < MEMBERS else nc.gpsimd
+            queue.dma_start(weight[:], member[0, j * EDGES : (j + 1) * EDGES].partition_broadcast(P))
+            weights.append(weight)
 
         windows = []
         for b in range(blocks):
             window = held.tile([P, EDGES], F32, name=f"window{b}")
-            nc.scalar.dma_start(window[:], hg[b * P : (b + 1) * P, :])
+            queue = nc.scalar if b == 0 else nc.gpsimd
+            queue.dma_start(window[:], hg[b * P : (b + 1) * P, :])
             windows.append(window)
 
-        def look_up(b, q, r):
+        def look_up(b, q):
             products = []
             for k in range(MEMBERS):
-                start = first_entry(q, k, r)
-                product = work.tile([P, PIECE], F32, name=f"product{k}")
+                j = q * MEMBERS + k
+                product = work.tile([P, EDGES], F32, name=f"product{k}")
                 nc.vector.tensor_tensor(
                     product[:],
-                    windows[b][:].indirect(offsets[:, start // PER_COLUMN : (start + PIECE) // PER_COLUMN]),
-                    weights[start][:],
+                    windows[b][:].indirect(offsets[:, j * columns : (j + 1) * columns]),
+                    weights[j][:],
                     MULT,
                 )
                 products.append(product)
             return products
 
-        def unite(b, q, r, products):
-            union = work.tile([P, PIECE], F32, name="union")
+        def unite(b, q, products):
+            union = work.tile([P, EDGES], F32, name="union")
             nc.vector.tensor_tensor(union[:], products[0][:], products[1][:], MAX)
-            column = q * EDGES + r * PIECE
-            nc.sync.dma_start(out[b * P : (b + 1) * P, column : column + PIECE], union[:])
+            nc.sync.dma_start(out[b * P : (b + 1) * P, q * EDGES : (q + 1) * EDGES], union[:])
 
-        steps = [(b, q, r) for b in range(blocks) for q in range(COALITIONS) for r in range(RUNS)]
+        steps = [(b, q) for b in range(blocks) for q in range(COALITIONS)]
         waiting = None
-        for b, q, r in steps:
-            products = look_up(b, q, r)
+        for b, q in steps:
+            products = look_up(b, q)
             if waiting is not None:
                 unite(*waiting)
-            waiting = (b, q, r, products)
+            waiting = (b, q, products)
         unite(*waiting)

@@ -30,14 +30,13 @@ def tile_position_game_kernel(tc, hg, member, offs, out):
         weights = []
         for j in range(pieces):
             weight = held.tile([P, EDGES], F32, name=f"weight{j}")
-            queue = nc.sync if j < MEMBERS else nc.gpsimd
-            queue.dma_start(weight[:], member[0, j * EDGES : (j + 1) * EDGES].partition_broadcast(P))
+            nc.sync.dma_start(weight[:], member[0, j * EDGES : (j + 1) * EDGES].partition_broadcast(P))
             weights.append(weight)
 
         windows = []
         for b in range(blocks):
             window = held.tile([P, EDGES], F32, name=f"window{b}")
-            queue = nc.scalar if b == 0 else nc.gpsimd
+            queue = nc.scalar if b == 0 else nc.sync
             queue.dma_start(window[:], hg[b * P : (b + 1) * P, :])
             windows.append(window)
 

@@ -21,7 +21,7 @@ def tile_position_game_kernel(tc, hg, member, offs, out):
     columns = EDGES // PER_COLUMN
     with (
         tc.tile_pool(name="held", bufs=1) as held,
-        tc.tile_pool(name="work", bufs=3) as work,
+        tc.tile_pool(name="work", bufs=2) as work,
     ):
         offsets = held.tile([P, LIST // PER_COLUMN], U16, name="offsets")
         nc.sync.dma_start(offsets[:], offs)
@@ -40,30 +40,28 @@ def tile_position_game_kernel(tc, hg, member, offs, out):
             queue.dma_start(window[:], hg[b * P : (b + 1) * P, :])
             windows.append(window)
 
-        def look_up(b, q):
-            products = []
+        def look_up(b, q, products):
             for k in range(MEMBERS):
                 j = q * MEMBERS + k
-                product = work.tile([P, EDGES], F32, name=f"product{k}")
                 nc.vector.tensor_tensor(
-                    product[:],
+                    products[k][:, q * EDGES : (q + 1) * EDGES],
                     windows[b][:].indirect(offsets[:, j * columns : (j + 1) * columns]),
                     weights[j][:],
                     MULT,
                 )
-                products.append(product)
-            return products
 
-        def unite(b, q, products):
-            union = work.tile([P, EDGES], F32, name="union")
-            nc.vector.tensor_tensor(union[:], products[0][:], products[1][:], MAX)
-            nc.sync.dma_start(out[b * P : (b + 1) * P, q * EDGES : (q + 1) * EDGES], union[:])
+        def unite(b, products, union, lo, hi):
+            nc.vector.tensor_tensor(union[:, lo:hi], products[0][:, lo:hi], products[1][:, lo:hi], MAX)
+            nc.sync.dma_start(out[b * P : (b + 1) * P, lo:hi], union[:, lo:hi])
 
-        steps = [(b, q) for b in range(blocks) for q in range(COALITIONS)]
         waiting = None
-        for b, q in steps:
-            products = look_up(b, q)
+        for b in range(blocks):
+            products = [work.tile([P, COALITIONS * EDGES], F32, name=f"product{k}") for k in range(MEMBERS)]
+            union = work.tile([P, COALITIONS * EDGES], F32, name="union")
+            look_up(b, 0, products)
             if waiting is not None:
-                unite(*waiting)
-            waiting = (b, q, products)
-        unite(*waiting)
+                unite(*waiting, 0, COALITIONS * EDGES)
+            look_up(b, 1, products)
+            waiting = (b, products, union)
+        for q in range(COALITIONS):
+            unite(*waiting, q * EDGES, (q + 1) * EDGES)

@@ -50,9 +50,9 @@ def tile_position_game_kernel(tc, hg, member, offs, out):
                     MULT,
                 )
 
-        def unite(b, products, union, lo, hi):
+        def unite(b, products, union, lo, hi, queue):
             nc.vector.tensor_tensor(union[:, lo:hi], products[0][:, lo:hi], products[1][:, lo:hi], MAX)
-            nc.sync.dma_start(out[b * P : (b + 1) * P, lo:hi], union[:, lo:hi])
+            queue.dma_start(out[b * P : (b + 1) * P, lo:hi], union[:, lo:hi])
 
         waiting = None
         for b in range(blocks):
@@ -60,8 +60,10 @@ def tile_position_game_kernel(tc, hg, member, offs, out):
             union = work.tile([P, COALITIONS * EDGES], F32, name="union")
             look_up(b, 0, products)
             if waiting is not None:
-                unite(*waiting, 0, COALITIONS * EDGES)
+                unite(*waiting, 0, COALITIONS * EDGES, nc.sync)
             look_up(b, 1, products)
             waiting = (b, products, union)
-        for q in range(COALITIONS):
-            unite(*waiting, q * EDGES, (q + 1) * EDGES)
+        half, three_quarters, whole = EDGES, EDGES + EDGES // 2, COALITIONS * EDGES
+        unite(*waiting, 0, half, nc.sync)
+        unite(*waiting, half, three_quarters, nc.scalar)
+        unite(*waiting, three_quarters, whole, nc.sync)

@@ -12,6 +12,7 @@ COALITIONS = 2
 MEMBERS = 2
 LIST = COALITIONS * MEMBERS * EDGES
 PER_COLUMN = 16
+LAST_RUNS = 4
 
 
 def tile_position_game_kernel(tc, hg, member, offs, out):
@@ -40,30 +41,32 @@ def tile_position_game_kernel(tc, hg, member, offs, out):
             queue.dma_start(window[:], hg[b * P : (b + 1) * P, :])
             windows.append(window)
 
-        def look_up(b, q, products):
-            for k in range(MEMBERS):
-                j = q * MEMBERS + k
-                nc.vector.tensor_tensor(
-                    products[k][:, q * EDGES : (q + 1) * EDGES],
-                    windows[b][:].indirect(offsets[:, j * columns : (j + 1) * columns]),
-                    weights[j][:],
-                    MULT,
-                )
+        def look_up(b, q, k, products):
+            j = q * MEMBERS + k
+            nc.vector.tensor_tensor(
+                products[k][:, q * EDGES : (q + 1) * EDGES],
+                windows[b][:].indirect(offsets[:, j * columns : (j + 1) * columns]),
+                weights[j][:],
+                MULT,
+            )
 
         def unite(b, products, union, lo, hi, queue):
             nc.vector.tensor_tensor(union[:, lo:hi], products[0][:, lo:hi], products[1][:, lo:hi], MAX)
             queue.dma_start(out[b * P : (b + 1) * P, lo:hi], union[:, lo:hi])
 
-        waiting = None
+        previous = None
         for b in range(blocks):
             products = [work.tile([P, COALITIONS * EDGES], F32, name=f"product{k}") for k in range(MEMBERS)]
             union = work.tile([P, COALITIONS * EDGES], F32, name="union")
-            look_up(b, 0, products)
-            if waiting is not None:
-                unite(*waiting, 0, COALITIONS * EDGES, nc.sync)
-            look_up(b, 1, products)
-            waiting = (b, products, union)
-        half, three_quarters, whole = EDGES, EDGES + EDGES // 2, COALITIONS * EDGES
-        unite(*waiting, 0, half, nc.sync)
-        unite(*waiting, half, three_quarters, nc.scalar)
-        unite(*waiting, three_quarters, whole, nc.sync)
+            look_up(b, 0, 0, products)
+            look_up(b, 0, 1, products)
+            if previous is not None:
+                unite(*previous, 0, COALITIONS * EDGES, nc.sync)
+            look_up(b, 1, 0, products)
+            if b == blocks - 1:
+                unite(b, products, union, 0, EDGES, nc.sync)
+            look_up(b, 1, 1, products)
+            previous = (b, products, union)
+        width = EDGES // LAST_RUNS
+        for r in range(LAST_RUNS):
+            unite(*previous, EDGES + r * width, EDGES + (r + 1) * width, nc.scalar if r % 2 == 0 else nc.sync)

@@ -12,7 +12,7 @@ COALITIONS = 2
 MEMBERS = 2
 LIST = COALITIONS * MEMBERS * EDGES
 PER_COLUMN = 16
-LAST_RUNS = 4
+LAST_RUNS = 2
 
 
 def tile_position_game_kernel(tc, hg, member, offs, out):

@@ -12,7 +12,7 @@ COALITIONS = 2
 MEMBERS = 2
 LIST = COALITIONS * MEMBERS * EDGES
 PER_COLUMN = 16
-LAST_RUNS = 2
+LAST_RUNS = 4
 
 
 def tile_position_game_kernel(tc, hg, member, offs, out):
@@ -54,6 +54,10 @@ def tile_position_game_kernel(tc, hg, member, offs, out):
             nc.vector.tensor_tensor(union[:, lo:hi], products[0][:, lo:hi], products[1][:, lo:hi], MAX)
             queue.dma_start(out[b * P : (b + 1) * P, lo:hi], union[:, lo:hi])
 
+        def last_run(r, b, products, union):
+            width = COALITIONS * EDGES // LAST_RUNS
+            unite(b, products, union, r * width, (r + 1) * width, nc.sync if r % 2 == 0 else nc.scalar)
+
         previous = None
         for b in range(blocks):
             products = [work.tile([P, COALITIONS * EDGES], F32, name=f"product{k}") for k in range(MEMBERS)]
@@ -64,9 +68,8 @@ def tile_position_game_kernel(tc, hg, member, offs, out):
                 unite(*previous, 0, COALITIONS * EDGES, nc.sync)
             look_up(b, 1, 0, products)
             if b == blocks - 1:
-                unite(b, products, union, 0, EDGES, nc.sync)
+                last_run(0, b, products, union)
             look_up(b, 1, 1, products)
             previous = (b, products, union)
-        width = EDGES // LAST_RUNS
-        for r in range(LAST_RUNS):
-            unite(*previous, EDGES + r * width, EDGES + (r + 1) * width, nc.scalar if r % 2 == 0 else nc.sync)
+        for r in range(1, LAST_RUNS):
+            last_run(r, *previous)

@@ -28,18 +28,21 @@ def tile_position_game_kernel(tc, hg, member, offs, out):
         nc.sync.dma_start(offsets[:], offs)
 
 
-        weights = []
-        for j in range(pieces):
-            weight = held.tile([P, EDGES], F32, name=f"weight{j}")
-            nc.sync.dma_start(weight[:], member[0, j * EDGES : (j + 1) * EDGES].partition_broadcast(P))
-            weights.append(weight)
+        weights = [held.tile([P, EDGES], F32, name=f"weight{j}") for j in range(pieces)]
+        windows = [held.tile([P, EDGES], F32, name=f"window{b}") for b in range(blocks)]
 
-        windows = []
-        for b in range(blocks):
-            window = held.tile([P, EDGES], F32, name=f"window{b}")
-            queue = nc.scalar if b == 0 else nc.sync
-            queue.dma_start(window[:], hg[b * P : (b + 1) * P, :])
-            windows.append(window)
+        def load_weight(j):
+            nc.sync.dma_start(weights[j][:], member[0, j * EDGES : (j + 1) * EDGES].partition_broadcast(P))
+
+        def load_window(b):
+            nc.sync.dma_start(windows[b][:], hg[b * P : (b + 1) * P, :])
+
+        load_weight(0)
+        load_window(0)
+        for j in range(1, pieces):
+            load_weight(j)
+        for b in range(1, blocks):
+            load_window(b)
 
         def look_up(b, q, k, products):
             j = q * MEMBERS + k

@@ -13,6 +13,9 @@ MEMBERS = 2
 LIST = COALITIONS * MEMBERS * EDGES
 PER_COLUMN = 16
 LAST_RUNS = 4
+FIRST_RUNS = 4
+
+FLOPS = NODES * LIST + NODES * COALITIONS * EDGES
 
 
 def tile_position_game_kernel(tc, hg, member, offs, out):
@@ -23,7 +26,13 @@ def tile_position_game_kernel(tc, hg, member, offs, out):
     with (
         tc.tile_pool(name="held", bufs=1) as held,
         tc.tile_pool(name="work", bufs=2) as work,
+        tc.psum_pool(name="psum", bufs=2) as psum,
     ):
+        row = held.tile([1, EDGES], F32, name="row")
+        nc.sync.dma_start(row[:], member[:, 0:EDGES])
+        ones = held.tile([1, P], F32, name="ones")
+        nc.vector.memset(ones[:], 1.0)
+
         offsets = held.tile([P, LIST // PER_COLUMN], U16, name="offsets")
         nc.sync.dma_start(offsets[:], offs)
 
@@ -37,21 +46,29 @@ def tile_position_game_kernel(tc, hg, member, offs, out):
         def load_window(b):
             nc.sync.dma_start(windows[b][:], hg[b * P : (b + 1) * P, :])
 
-        load_weight(0)
         load_window(0)
         for j in range(1, pieces):
             load_weight(j)
         for b in range(1, blocks):
             load_window(b)
 
-        def look_up(b, q, k, products):
+        run = EDGES // FIRST_RUNS
+        for r in range(FIRST_RUNS):
+            bank = psum.tile([P, run], F32, name="bank")
+            nc.tensor.matmul(bank[:], ones[:], row[:, r * run : (r + 1) * run], start=True, stop=True)
+            nc.scalar.copy(weights[0][:, r * run : (r + 1) * run], bank[:])
+
+        def look_up(b, q, k, products, runs=1):
             j = q * MEMBERS + k
-            nc.vector.tensor_tensor(
-                products[k][:, q * EDGES : (q + 1) * EDGES],
-                windows[b][:].indirect(offsets[:, j * columns : (j + 1) * columns]),
-                weights[j][:],
-                MULT,
-            )
+            width = EDGES // runs
+            for r in range(runs):
+                lo, hi = r * width, (r + 1) * width
+                nc.vector.tensor_tensor(
+                    products[k][:, q * EDGES + lo : q * EDGES + hi],
+                    windows[b][:].indirect(offsets[:, j * columns + lo // PER_COLUMN : j * columns + hi // PER_COLUMN]),
+                    weights[j][:, lo:hi],
+                    MULT,
+                )
 
         def unite(b, products, union, lo, hi, queue):
             nc.vector.tensor_tensor(union[:, lo:hi], products[0][:, lo:hi], products[1][:, lo:hi], MAX)
@@ -65,7 +82,7 @@ def tile_position_game_kernel(tc, hg, member, offs, out):
         for b in range(blocks):
             products = [work.tile([P, COALITIONS * EDGES], F32, name=f"product{k}") for k in range(MEMBERS)]
             union = work.tile([P, COALITIONS * EDGES], F32, name="union")
-            look_up(b, 0, 0, products)
+            look_up(b, 0, 0, products, runs=FIRST_RUNS if b == 0 else 1)
             look_up(b, 0, 1, products)
             if previous is not None:
                 unite(*previous, 0, COALITIONS * EDGES, nc.sync)

@@ -14,6 +14,7 @@ LIST = COALITIONS * MEMBERS * EDGES
 PER_COLUMN = 16
 LAST_RUNS = 4
 FIRST_RUNS = 4
+DEPTH = 2
 
 FLOPS = NODES * LIST + NODES * COALITIONS * EDGES
 
@@ -22,10 +23,9 @@ def tile_position_game_kernel(tc, hg, member, offs, out):
     nc = tc.nc
     blocks = NODES // P
     pieces = COALITIONS * MEMBERS
-    columns = EDGES // PER_COLUMN
     with (
         tc.tile_pool(name="held", bufs=1) as held,
-        tc.tile_pool(name="work", bufs=2) as work,
+        tc.tile_pool(name="work", bufs=DEPTH) as work,
         tc.psum_pool(name="psum", bufs=2) as psum,
     ):
         row = held.tile([1, EDGES], F32, name="row")
@@ -36,7 +36,6 @@ def tile_position_game_kernel(tc, hg, member, offs, out):
         offsets = held.tile([P, LIST // PER_COLUMN], U16, name="offsets")
         nc.sync.dma_start(offsets[:], offs)
 
-
         weights = [held.tile([P, EDGES], F32, name=f"weight{j}") for j in range(pieces)]
         windows = [held.tile([P, EDGES], F32, name=f"window{b}") for b in range(blocks)]
 
@@ -46,29 +45,26 @@ def tile_position_game_kernel(tc, hg, member, offs, out):
         def load_window(b):
             nc.sync.dma_start(windows[b][:], hg[b * P : (b + 1) * P, :])
 
-        load_window(0)
+        for b in range(DEPTH):
+            load_window(b)
         for j in range(1, pieces):
             load_weight(j)
-        for b in range(1, blocks):
+        for b in range(DEPTH, blocks):
             load_window(b)
 
-        run = EDGES // FIRST_RUNS
-        for r in range(FIRST_RUNS):
-            bank = psum.tile([P, run], F32, name="bank")
-            nc.tensor.matmul(bank[:], ones[:], row[:, r * run : (r + 1) * run], start=True, stop=True)
-            nc.scalar.copy(weights[0][:, r * run : (r + 1) * run], bank[:])
+        def new_block():
+            products = [work.tile([P, COALITIONS * EDGES], F32, name=f"product{k}") for k in range(MEMBERS)]
+            union = work.tile([P, COALITIONS * EDGES], F32, name="union")
+            return products, union
 
-        def look_up(b, q, k, products, runs=1):
-            j = q * MEMBERS + k
-            width = EDGES // runs
-            for r in range(runs):
-                lo, hi = r * width, (r + 1) * width
-                nc.vector.tensor_tensor(
-                    products[k][:, q * EDGES + lo : q * EDGES + hi],
-                    windows[b][:].indirect(offsets[:, j * columns + lo // PER_COLUMN : j * columns + hi // PER_COLUMN]),
-                    weights[j][:, lo:hi],
-                    MULT,
-                )
+        def look_up(b, q, k, products, lo=0, hi=EDGES):
+            start = (q * MEMBERS + k) * EDGES
+            nc.vector.tensor_tensor(
+                products[k][:, q * EDGES + lo : q * EDGES + hi],
+                windows[b][:].indirect(offsets[:, (start + lo) // PER_COLUMN : (start + hi) // PER_COLUMN]),
+                weights[q * MEMBERS + k][:, lo:hi],
+                MULT,
+            )
 
         def unite(b, products, union, lo, hi, queue):
             nc.vector.tensor_tensor(union[:, lo:hi], products[0][:, lo:hi], products[1][:, lo:hi], MAX)
@@ -78,11 +74,23 @@ def tile_position_game_kernel(tc, hg, member, offs, out):
             width = COALITIONS * EDGES // LAST_RUNS
             unite(b, products, union, r * width, (r + 1) * width, nc.sync if r % 2 == 0 else nc.scalar)
 
+        early = [new_block() for b in range(DEPTH)]
+        width = EDGES // FIRST_RUNS
+        for r in range(FIRST_RUNS):
+            lo, hi = r * width, (r + 1) * width
+            bank = psum.tile([P, width], F32, name="bank")
+            nc.tensor.matmul(bank[:], ones[:], row[:, lo:hi], start=True, stop=True)
+            nc.scalar.copy(weights[0][:, lo:hi], bank[:])
+            for b in range(DEPTH):
+                look_up(b, 0, 0, early[b][0], lo, hi)
+
         previous = None
         for b in range(blocks):
-            products = [work.tile([P, COALITIONS * EDGES], F32, name=f"product{k}") for k in range(MEMBERS)]
-            union = work.tile([P, COALITIONS * EDGES], F32, name="union")
-            look_up(b, 0, 0, products, runs=FIRST_RUNS if b == 0 else 1)
+            if b < DEPTH:
+                products, union = early[b]
+            else:
+                products, union = new_block()
+                look_up(b, 0, 0, products)
             look_up(b, 0, 1, products)
             if previous is not None:
                 unite(*previous, 0, COALITIONS * EDGES, nc.sync)

@@ -66,13 +66,13 @@ def tile_position_game_kernel(tc, hg, member, offs, out):
                 MULT,
             )
 
-        def unite(b, products, union, lo, hi, queue):
+        def unite(b, products, union, lo, hi):
             nc.vector.tensor_tensor(union[:, lo:hi], products[0][:, lo:hi], products[1][:, lo:hi], MAX)
-            queue.dma_start(out[b * P : (b + 1) * P, lo:hi], union[:, lo:hi])
+            nc.sync.dma_start(out[b * P : (b + 1) * P, lo:hi], union[:, lo:hi])
 
         def last_run(r, b, products, union):
             width = COALITIONS * EDGES // LAST_RUNS
-            unite(b, products, union, r * width, (r + 1) * width, nc.sync if r % 2 == 0 else nc.scalar)
+            unite(b, products, union, r * width, (r + 1) * width)
 
         early = [new_block() for b in range(DEPTH)]
         width = EDGES // FIRST_RUNS
@@ -93,7 +93,7 @@ def tile_position_game_kernel(tc, hg, member, offs, out):
                 look_up(b, 0, 0, products)
             look_up(b, 0, 1, products)
             if previous is not None:
-                unite(*previous, 0, COALITIONS * EDGES, nc.sync)
+                unite(*previous, 0, COALITIONS * EDGES)
             look_up(b, 1, 0, products)
             if b == blocks - 1:
                 last_run(0, b, products, union)

@@ -80,7 +80,10 @@ def tile_position_game_kernel(tc, hg, member, offs, out):
             lo, hi = r * width, (r + 1) * width
             bank = psum.tile([P, width], F32, name="bank")
             nc.tensor.matmul(bank[:], ones[:], row[:, lo:hi], start=True, stop=True)
-            nc.scalar.copy(weights[0][:, lo:hi], bank[:])
+            if r == 0:
+                nc.vector.tensor_copy(weights[0][:, lo:hi], bank[:])
+            else:
+                nc.scalar.copy(weights[0][:, lo:hi], bank[:])
             for b in range(DEPTH):
                 look_up(b, 0, 0, early[b][0], lo, hi)
 

@@ -84,8 +84,12 @@ def tile_position_game_kernel(tc, hg, member, offs, out):
                 nc.vector.tensor_copy(weights[0][:, lo:hi], bank[:])
             else:
                 nc.scalar.copy(weights[0][:, lo:hi], bank[:])
+        look_up(0, 0, 0, early[0][0], 0, width)
+        look_up(0, 0, 0, early[0][0], width, 2 * width)
+        look_up(1, 0, 0, early[1][0], 0, 2 * width)
+        for r in range(2, FIRST_RUNS):
             for b in range(DEPTH):
-                look_up(b, 0, 0, early[b][0], lo, hi)
+                look_up(b, 0, 0, early[b][0], r * width, (r + 1) * width)
 
         previous = None
         for b in range(blocks):

@@ -91,16 +91,17 @@ def tile_position_game_kernel(tc, hg, member, offs, out):
             for b in range(DEPTH):
                 look_up(b, 0, 0, early[b][0], r * width, (r + 1) * width)
 
-        previous = None
-        for b in range(blocks):
-            if b < DEPTH:
-                products, union = early[b]
-            else:
-                products, union = new_block()
-                look_up(b, 0, 0, products)
+        for j in range(1, pieces):
+            for b in range(DEPTH):
+                look_up(b, j // MEMBERS, j % MEMBERS, early[b][0])
+
+        unite(0, early[0][0], early[0][1], 0, COALITIONS * EDGES)
+        previous = (1, early[1][0], early[1][1])
+        for b in range(DEPTH, blocks):
+            products, union = new_block()
+            look_up(b, 0, 0, products)
             look_up(b, 0, 1, products)
-            if previous is not None:
-                unite(*previous, 0, COALITIONS * EDGES)
+            unite(*previous, 0, COALITIONS * EDGES)
             look_up(b, 1, 0, products)
             if b == blocks - 1:
                 last_run(0, b, products, union)

import concourse.mybir as mybir

F32 = mybir.dt.float32
U16 = mybir.dt.uint16
MULT = mybir.AluOpType.mult
MAX = mybir.AluOpType.max

P = 128
NODES = 512
EDGES = 1024
COALITIONS = 2
MEMBERS = 2
LIST = COALITIONS * MEMBERS * EDGES
PER_COLUMN = 16
LAST_RUNS = 4
FIRST_RUNS = 4
DEPTH = 2

FLOPS = NODES * LIST + NODES * COALITIONS * EDGES


def tile_position_game_kernel(tc, hg, member, offs, out):
    nc = tc.nc
    blocks = NODES // P
    pieces = COALITIONS * MEMBERS
    with (
        tc.tile_pool(name="held", bufs=1) as held,
        tc.tile_pool(name="work", bufs=DEPTH) as work,
        tc.psum_pool(name="psum", bufs=2) as psum,
    ):
        row = held.tile([1, EDGES], F32, name="row")
        nc.sync.dma_start(row[:], member[:, 0:EDGES])
        ones = held.tile([1, P], F32, name="ones")
        nc.vector.memset(ones[:], 1.0)

        offsets = held.tile([P, LIST // PER_COLUMN], U16, name="offsets")
        nc.sync.dma_start(offsets[:], offs)

        weights = [held.tile([P, EDGES], F32, name=f"weight{j}") for j in range(pieces)]
        windows = [held.tile([P, EDGES], F32, name=f"window{b}") for b in range(blocks)]

        def load_weight(j):
            nc.sync.dma_start(weights[j][:], member[0, j * EDGES : (j + 1) * EDGES].partition_broadcast(P))

        def load_window(b):
            nc.sync.dma_start(windows[b][:], hg[b * P : (b + 1) * P, :])

        for b in range(DEPTH):
            load_window(b)
        for j in range(1, pieces):
            load_weight(j)
        for b in range(DEPTH, blocks):
            load_window(b)

        def new_block():
            products = [work.tile([P, COALITIONS * EDGES], F32, name=f"product{k}") for k in range(MEMBERS)]
            union = work.tile([P, COALITIONS * EDGES], F32, name="union")
            return products, union

        def look_up(b, q, k, products, lo=0, hi=EDGES):
            start = (q * MEMBERS + k) * EDGES
            nc.vector.tensor_tensor(
                products[k][:, q * EDGES + lo : q * EDGES + hi],
                windows[b][:].indirect(offsets[:, (start + lo) // PER_COLUMN : (start + hi) // PER_COLUMN]),
                weights[q * MEMBERS + k][:, lo:hi],
                MULT,
            )

        def unite(b, products, union, lo, hi):
            nc.vector.tensor_tensor(union[:, lo:hi], products[0][:, lo:hi], products[1][:, lo:hi], MAX)
            nc.sync.dma_start(out[b * P : (b + 1) * P, lo:hi], union[:, lo:hi])

        def last_run(r, b, products, union):
            width = COALITIONS * EDGES // LAST_RUNS
            unite(b, products, union, r * width, (r + 1) * width)

        early = [new_block() for b in range(DEPTH)]
        width = EDGES // FIRST_RUNS
        for r in range(FIRST_RUNS):
            lo, hi = r * width, (r + 1) * width
            bank = psum.tile([P, width], F32, name="bank")
            nc.tensor.matmul(bank[:], ones[:], row[:, lo:hi], start=True, stop=True)
            if r == 0:
                nc.vector.tensor_copy(weights[0][:, lo:hi], bank[:])
            else:
                nc.scalar.copy(weights[0][:, lo:hi], bank[:])
        look_up(0, 0, 0, early[0][0], 0, width)
        look_up(0, 0, 0, early[0][0], width, 2 * width)
        look_up(1, 0, 0, early[1][0], 0, 2 * width)
        for r in range(2, FIRST_RUNS):
            for b in range(DEPTH):
                look_up(b, 0, 0, early[b][0], r * width, (r + 1) * width)

        for j in range(1, pieces):
            for b in range(DEPTH):
                look_up(b, j // MEMBERS, j % MEMBERS, early[b][0])

        unite(0, early[0][0], early[0][1], 0, COALITIONS * EDGES)
        previous = (1, early[1][0], early[1][1])
        for b in range(DEPTH, blocks):
            products, union = new_block()
            look_up(b, 0, 0, products)
            look_up(b, 0, 1, products)
            unite(*previous, 0, COALITIONS * EDGES)
            look_up(b, 1, 0, products)
            if b == blocks - 1:
                last_run(0, b, products, union)
            look_up(b, 1, 1, products)
            previous = (b, products, union)
        for r in range(1, LAST_RUNS):
            last_run(r, *previous)
